import numpy as np
import ml_dtypes


def mxq(x, axis, fmt="e4m3"):
    dtype, down = {"e4m3": (ml_dtypes.float8_e4m3fn, 7), "e5m2": (ml_dtypes.float8_e5m2, 14)}[fmt]
    v = np.moveaxis(np.asarray(x, np.float32).astype(ml_dtypes.bfloat16).astype(np.float64), axis, -1)
    blocks = v.reshape(v.shape[:-1] + (-1, 32))
    amax = np.abs(blocks).max(-1, keepdims=True)
    byte = np.maximum(np.where(amax > 0, np.frexp(amax)[1] - 1 + 127, 0) - down, 1)
    scale = np.exp2(byte - 127.0)
    codes = (blocks / scale).astype(np.float32).astype(dtype).astype(np.float64)
    return np.moveaxis((codes * scale).reshape(v.shape), -1, axis)


WIDE = False


def mx_kscale(k):
    if not WIDE:
        return np.ones(k)
    levels = np.array([10, -10, 5, -5, 0])
    a = np.random.permutation(np.resize(levels, k // 512 * 4)).reshape(k // 512, 4)
    idx = np.arange(k)
    return np.exp2(a[idx // 512, idx % 128 // 32])


BF16 = ml_dtypes.bfloat16


def bf(x):
    return np.asarray(x, np.float32).astype(BF16)


def f64(x):
    return np.asarray(x).astype(np.float64)


B, T, C, H, D, R = 4, 1024, 1024, 4, 128, 512
EPS = 1e-6
THETA = 10000.0


def rmsnorm(v, w):
    var = np.mean(v * v, axis=-1, keepdims=True)
    return v * (1.0 / np.sqrt(var + EPS)) * w


def rope(v, cos, sin):
    re, im = v[..., 0::2], v[..., 1::2]
    c, s = cos[None, :, None, :], sin[None, :, None, :]
    return np.stack([re * c - im * s, re * s + im * c], axis=-1).reshape(v.shape)


def setup_inputs():
    s, t = mx_kscale(C), mx_kscale(R)
    ang = np.outer(np.arange(T), 1.0 / THETA ** (np.arange(0, D, 2) / D))
    return {"x": bf(np.random.standard_normal((B, T, C)) * s),
            "w_kv_down": bf(np.random.standard_normal((R, C)) / np.sqrt(C) / s[None, :] * t[:, None]),
            "w_kv_up": bf(np.random.standard_normal((2 * H * D, R)) / np.sqrt(R) / t[None, :]),
            "k_norm_w": bf(1.0 + 0.1 * np.random.standard_normal(D)),
            "freqs_cos": bf(np.cos(ang)), "freqs_sin": bf(np.sin(ang))}


def reference(x, w_kv_down, w_kv_up, k_norm_w, freqs_cos, freqs_sin):
    latent = mxq(f64(x), 2, "e4m3") @ mxq(f64(w_kv_down), 1, "e4m3").T
    kv = (mxq(latent, 2, "e4m3") @ mxq(f64(w_kv_up), 1, "e4m3").T).reshape(B, T, 2, H, D)
    xk, xv = kv[:, :, 0], kv[:, :, 1]
    return rope(rmsnorm(xk, f64(k_norm_w)), f64(freqs_cos), f64(freqs_sin)), xv

@@ -1,0 +1,260 @@
+from contextlib import ExitStack
+
+import concourse.mybir as mybir
+from concourse.masks import make_identity
+
+F32 = mybir.dt.float32
+BF16 = mybir.dt.bfloat16
+U32 = mybir.dt.uint32
+U8 = mybir.dt.uint8
+FP8X4 = mybir.dt.float8_e4m3fn_x4
+ALU = mybir.AluOpType
+ACT = mybir.ActivationFunctionType
+
+P = 128
+PACK = 4
+K_PASS = P * PACK
+
+TOKENS = 4 * 1024
+SEQ = 1024
+C = 1024
+R = 512
+HEADS = 4
+D = 128
+HALF_D = D // 2
+KEY_COLS = HEADS * D
+EPS = 1e-6
+
+C_PASSES = C // K_PASS
+TILES = 2
+STEP_TOKENS = TILES * P
+STEPS = TOKENS // STEP_TOKENS
+SEQ_TILES = SEQ // P
+
+FLOPS = 2 * TOKENS * C * R + 2 * TOKENS * R * 2 * KEY_COLS
+
+
+def twins_to_partitions(nc, psum, identity, twin_blocks, grouped, copy_out):
+    bank = psum.tile([P, 2, 2, P], F32, tag="twins")
+    for a in range(2):
+        for u in range(2):
+            nc.tensor.transpose(bank[:, a, u, :], twin_blocks[a][u], identity)
+    copy_out(out=grouped, in_=bank[:].rearrange("q a u r -> q a r u"))
+
+
+def channel_blocks(rows):
+    twins = rows.bitcast(F32)
+    return [[twins[:, (2 * g + u) * P : (2 * g + u + 1) * P] for u in range(2)] for g in range(C_PASSES)]
+
+
+def tile_mla_pa_t_kernel(
+    tc, x, w_kv_down, w_kv_up, k_norm_w, freqs_cos, freqs_sin, out_0, out_1
+):
+    nc = tc.nc
+    x_rows = x.flatten_outer_dims()
+    k_rows = out_0.rearrange("b t h d -> (b t) (h d)")
+    v_rows = out_1.rearrange("b t h d -> (b t) (h d)")
+
+    with ExitStack() as pools:
+        const = pools.enter_context(tc.tile_pool(name="const", bufs=1))
+        x_pool = pools.enter_context(tc.tile_pool(name="x", bufs=STEPS))
+        step_pool = pools.enter_context(tc.tile_pool(name="step", bufs=3))
+        tile_pool = pools.enter_context(tc.tile_pool(name="tile", bufs=4))
+        psum = pools.enter_context(tc.psum_pool(name="psum", bufs=2))
+
+        wd_sb = const.tile([P, PACK, C], BF16)
+        nc.sync.dma_start(out=wd_sb[:], in_=w_kv_down.rearrange("(p t) c -> p t c", t=PACK))
+        wu_sb = const.tile([P, 2 * HEADS, R], BF16)
+        x_sb = []
+        for s in range(STEPS):
+            x_step = x_pool.tile([P, TILES, C], BF16)
+            nc.sync.dma_start(
+                out=x_step[:],
+                in_=x_rows[s * STEP_TOKENS : (s + 1) * STEP_TOKENS, :].rearrange("(p n) c -> p n c", n=TILES),
+            )
+            x_sb.append(x_step)
+            if s == 0:
+                nc.sync.dma_start(out=wu_sb[:], in_=w_kv_up.rearrange("(b p) r -> p b r", p=P))
+
+        cos_sb = const.tile([P, SEQ_TILES, HALF_D], BF16)
+        sin_sb = const.tile([P, SEQ_TILES, HALF_D], BF16)
+        gain_sb = const.tile([P, HALF_D, 2], BF16)
+        nc.scalar.dma_start(
+            out=cos_sb[:].rearrange("p (s n) j -> p s n j", n=TILES),
+            in_=freqs_cos.rearrange("(s p n) j -> p s n j", p=P, n=TILES),
+        )
+        nc.scalar.dma_start(
+            out=sin_sb[:].rearrange("p (s n) j -> p s n j", n=TILES),
+            in_=freqs_sin.rearrange("(s p n) j -> p s n j", p=P, n=TILES),
+        )
+        nc.scalar.dma_start(out=gain_sb[:].rearrange("p j e -> p (j e)"), in_=k_norm_w.partition_broadcast(P))
+
+        identity = const.tile([P, P], F32)
+        make_identity(nc, identity[:])
+        eps = const.tile([P, 1], F32)
+        nc.vector.memset(eps[:], EPS)
+        table_warmer = const.tile([P, 1], F32)
+        nc.scalar.activation(out=table_warmer[:], in_=eps[:], func=ACT.Sqrt)
+
+        partner_gain = const.tile([P, HALF_D, 2], F32)
+        nc.gpsimd.tensor_scalar_mul(out=partner_gain[:, :, 0], in0=gain_sb[:, :, 1], scalar1=-1.0)
+        nc.gpsimd.tensor_copy(out=partner_gain[:, :, 1], in_=gain_sb[:, :, 0])
+        own_table = const.tile([P, SEQ_TILES, HALF_D, 2], F32)
+        partner_table = const.tile([P, SEQ_TILES, HALF_D, 2], F32)
+        table_shape = [P, SEQ_TILES, HALF_D, 2]
+        nc.gpsimd.tensor_tensor(
+            out=own_table[:],
+            in0=cos_sb[:].unsqueeze(3).to_broadcast(table_shape),
+            in1=gain_sb[:].unsqueeze(1).to_broadcast(table_shape),
+            op=ALU.mult,
+        )
+        nc.gpsimd.tensor_tensor(
+            out=partner_table[:],
+            in0=sin_sb[:].unsqueeze(3).to_broadcast(table_shape),
+            in1=partner_gain[:].unsqueeze(1).to_broadcast(table_shape),
+            op=ALU.mult,
+        )
+
+        wd_grouped = const.tile([P, PACK * C_PASSES * P * PACK], BF16, align_bytes=64)
+        wd_codes = const.tile([P, PACK, C_PASSES, P], U32, align_bytes=64)
+        wd_scales = const.tile([P, PACK, C_PASSES, P], U8, align_bytes=64)
+        wd_grouped_twins = wd_grouped[:].bitcast(F32).rearrange("q (t g r u) -> q t g r u", t=PACK, g=C_PASSES, u=2)
+        for t in range(PACK):
+            twins_to_partitions(
+                nc, psum, identity[:], channel_blocks(wd_sb[:, t, :]), wd_grouped_twins[:, t], nc.vector.tensor_copy
+            )
+        nc.vector.quantize_mx(
+            out=wd_codes[:].rearrange("q t g r -> q (t g r)").bitcast(FP8X4),
+            scales=wd_scales[:].rearrange("q t g r -> q (t g r)"),
+            in_=wd_grouped[:],
+        )
+
+        def quantise_w_kv_up():
+            grouped = const.tile([P, 2 * KEY_COLS * PACK], BF16, align_bytes=64, name="wu_grouped")
+            grouped_twins = grouped[:].bitcast(F32).rearrange("q (c a r u) -> q c a r u", a=2, r=P, u=2)
+            for c in range(HEADS):
+                blocks = [
+                    [wu_sb[:, 2 * c + a, :].bitcast(F32).rearrange("o (q u) -> o u q", u=2)[:, u, :] for u in range(2)]
+                    for a in range(2)
+                ]
+                twins_to_partitions(nc, psum, identity[:], blocks, grouped_twins[:, c], nc.vector.tensor_copy)
+            nc.vector.quantize_mx(out=wu_codes[:].bitcast(FP8X4), scales=wu_scales[:], in_=grouped[:])
+
+        wu_codes = const.tile([P, 2 * KEY_COLS], U32, align_bytes=64)
+        wu_scales = const.tile([P, 2 * KEY_COLS], U8, align_bytes=64)
+
+        def quantise_x(s):
+            grouped = step_pool.tile([P, TILES * C_PASSES * P * PACK], BF16, align_bytes=64, name="x_grouped")
+            codes = step_pool.tile([P, TILES, C_PASSES, P], U32, align_bytes=64, name="x_codes")
+            scales = step_pool.tile([P, TILES, C_PASSES, P], U8, align_bytes=64, name="x_scales")
+            grouped_twins = grouped[:].bitcast(F32).rearrange("q (n g r u) -> q n g r u", n=TILES, g=C_PASSES, u=2)
+            for n in range(TILES):
+                twins_to_partitions(
+                    nc, psum, identity[:], channel_blocks(x_sb[s][:, n, :]), grouped_twins[:, n], nc.scalar.copy
+                )
+            nc.vector.quantize_mx(
+                out=codes[:].rearrange("q n g r -> q (n g r)").bitcast(FP8X4),
+                scales=scales[:].rearrange("q n g r -> q (n g r)"),
+                in_=grouped[:],
+            )
+            return codes, scales
+
+        def quantised_latent(x_codes, x_scales):
+            grouped = step_pool.tile([P, TILES, P, PACK], BF16, align_bytes=64, name="latent_grouped")
+            codes = step_pool.tile([P, TILES, P], U32, align_bytes=64, name="latent_codes")
+            scales = step_pool.tile([P, TILES, P], U8, align_bytes=64, name="latent_scales")
+            for n in range(TILES):
+                latent_ps = psum.tile([P, PACK, P], F32, tag="latent")
+                for t in range(PACK):
+                    for g in range(C_PASSES):
+                        nc.tensor.matmul_mx(
+                            out=latent_ps[:, t, :],
+                            lhsT=wd_codes[:, t, g, :].bitcast(FP8X4),
+                            lhsT_scale=wd_scales[:, t, g, :],
+                            rhs=x_codes[:, n, g, :].bitcast(FP8X4),
+                            rhs_scale=x_scales[:, n, g, :],
+                            start=(g == 0),
+                            stop=(g == C_PASSES - 1),
+                        )
+                nc.scalar.copy(out=grouped[:, n, :, :], in_=latent_ps[:].rearrange("p t r -> p r t"))
+            nc.vector.quantize_mx(
+                out=codes[:].rearrange("p n r -> p (n r)").bitcast(FP8X4),
+                scales=scales[:].rearrange("p n r -> p (n r)"),
+                in_=grouped[:].rearrange("p n r t -> p (n r t)"),
+            )
+            return codes, scales
+
+        def keys_and_values(s, latent_codes, latent_scales):
+            k_out = step_pool.tile([P, TILES, KEY_COLS], F32)
+            v_out = step_pool.tile([P, TILES, KEY_COLS], F32)
+            for n in range(TILES):
+                k_ps = psum.tile([P, HEADS, HALF_D, 2], F32, tag="k")
+                v_ps = psum.tile([P, KEY_COLS], F32, tag="v")
+                for half_ps, first_col in ((k_ps[:].rearrange("p h j e -> p (h j e)"), 0), (v_ps[:], KEY_COLS)):
+                    nc.tensor.matmul_mx(
+                        out=half_ps,
+                        lhsT=latent_codes[:, n, :].bitcast(FP8X4),
+                        lhsT_scale=latent_scales[:, n, :],
+                        rhs=wu_codes[:, first_col : first_col + KEY_COLS].bitcast(FP8X4),
+                        rhs_scale=wu_scales[:, first_col : first_col + KEY_COLS],
+                        start=True,
+                        stop=True,
+                    )
+
+                squares = tile_pool.tile([P, HEADS, HALF_D, 2], F32)
+                sum_squares = tile_pool.tile([P, HEADS], F32)
+                for h in range(HEADS):
+                    nc.scalar.activation(
+                        out=squares[:, h], in_=k_ps[:, h], func=ACT.Square, accum_out=sum_squares[:, h : h + 1]
+                    )
+                rms = tile_pool.tile([P, HEADS], F32)
+                nc.scalar.activation(out=rms[:], in_=sum_squares[:], func=ACT.Sqrt, scale=1.0 / D, bias=eps[:])
+                rstd = tile_pool.tile([P, HEADS], F32)
+                nc.vector.reciprocal(out=rstd[:], in_=rms[:])
+
+                if n % 2 == 0:
+                    nc.scalar.copy(out=v_out[:, n, :], in_=v_ps[:])
+                else:
+                    nc.vector.tensor_copy(out=v_out[:, n, :], in_=v_ps[:])
+
+                position = (s * TILES + n) % SEQ_TILES
+                own = tile_pool.tile([P, HEADS, HALF_D, 2], F32)
+                partner = tile_pool.tile([P, HEADS, HALF_D, 2], F32)
+                for h in range(HEADS):
+                    nc.vector.scalar_tensor_tensor(
+                        out=own[:, h],
+                        in0=k_ps[:, h],
+                        scalar=rstd[:, h : h + 1],
+                        in1=own_table[:, position],
+                        op0=ALU.mult,
+                        op1=ALU.mult,
+                    )
+                    nc.vector.scalar_tensor_tensor(
+                        out=partner[:, h],
+                        in0=k_ps[:, h, :, ::-1],
+                        scalar=rstd[:, h : h + 1],
+                        in1=partner_table[:, position],
+                        op0=ALU.mult,
+                        op1=ALU.mult,
+                    )
+                nc.gpsimd.tensor_tensor(
+                    out=k_out[:, n, :],
+                    in0=own[:].rearrange("p h j e -> p (h j e)"),
+                    in1=partner[:].rearrange("p h j e -> p (h j e)"),
+                    op=ALU.add,
+                )
+            step_rows = slice(s * STEP_TOKENS, (s + 1) * STEP_TOKENS)
+            nc.sync.dma_start(out=k_rows[step_rows, :].rearrange("(p n) f -> p n f", n=TILES), in_=k_out[:])
+            nc.sync.dma_start(out=v_rows[step_rows, :].rearrange("(p n) f -> p n f", n=TILES), in_=v_out[:])
+
+        x_quantised = {}
+        latent_quantised = {}
+        for i in range(STEPS + 2):
+            if i < STEPS:
+                x_quantised[i] = quantise_x(i)
+            if i == 0:
+                quantise_w_kv_up()
+            if 1 <= i <= STEPS:
+                latent_quantised[i - 1] = quantised_latent(*x_quantised[i - 1])
+            if i >= 2:
+                keys_and_values(i - 2, *latent_quantised[i - 2])

@@ -26,20 +26,28 @@ KEY_COLS = HEADS * D
 EPS = 1e-6
 
 C_PASSES = C // K_PASS
-TILES = 2
-STEP_TOKENS = TILES * P
-STEPS = TOKENS // STEP_TOKENS
+N_TILES = TOKENS // P
 SEQ_TILES = SEQ // P
+PAIR = 2
+N_PAIRS = N_TILES // PAIR
+
+LATENT_LAG = 1
+FINISH_LAG = 3
 
 FLOPS = 2 * TOKENS * C * R + 2 * TOKENS * R * 2 * KEY_COLS
 
 
-def twins_to_partitions(nc, psum, identity, twin_blocks, grouped, copy_out):
-    bank = psum.tile([P, 2, 2, P], F32, tag="twins")
+def transpose_twins(nc, bank, identity, twin_blocks):
     for a in range(2):
         for u in range(2):
             nc.tensor.transpose(bank[:, a, u, :], twin_blocks[a][u], identity)
-    copy_out(out=grouped, in_=bank[:].rearrange("q a u r -> q a r u"))
+
+
+def group_twins(copy_out, bank, grouped):
+    copy_out(
+        out=grouped[:].bitcast(F32).rearrange("q (a r u) -> q a r u", a=2, u=2),
+        in_=bank[:].rearrange("q a u r -> q a r u"),
+    )
 
 
 def channel_blocks(rows):
@@ -51,41 +59,39 @@ def tile_mla_pa_t_kernel(
     tc, x, w_kv_down, w_kv_up, k_norm_w, freqs_cos, freqs_sin, out_0, out_1
 ):
     nc = tc.nc
-    x_rows = x.flatten_outer_dims()
-    k_rows = out_0.rearrange("b t h d -> (b t) (h d)")
-    v_rows = out_1.rearrange("b t h d -> (b t) (h d)")
+    x_rows = x.flatten_outer_dims().rearrange("(s p n) c -> s p n c", p=P, n=PAIR)
+    k_rows = out_0.rearrange("b t h d -> (b t) (h d)").rearrange("(s p n) f -> s p n f", p=P, n=PAIR)
+    v_rows = out_1.rearrange("b t h d -> (b t) (h d)").rearrange("(s p n) f -> s p n f", p=P, n=PAIR)
 
-    with ExitStack() as pools:
-        const = pools.enter_context(tc.tile_pool(name="const", bufs=1))
-        x_pool = pools.enter_context(tc.tile_pool(name="x", bufs=STEPS))
-        step_pool = pools.enter_context(tc.tile_pool(name="step", bufs=3))
-        tile_pool = pools.enter_context(tc.tile_pool(name="tile", bufs=4))
-        psum = pools.enter_context(tc.psum_pool(name="psum", bufs=2))
+    with ExitStack() as stack:
+        stack.enter_context(tc.manual_schedule())
+        const = stack.enter_context(tc.tile_pool(name="const", bufs=1))
+        x_pool = stack.enter_context(tc.tile_pool(name="x", bufs=N_PAIRS))
+        work = stack.enter_context(tc.tile_pool(name="work", bufs=3))
+        psum = stack.enter_context(tc.psum_pool(name="psum", bufs=1))
 
         wd_sb = const.tile([P, PACK, C], BF16)
-        nc.sync.dma_start(out=wd_sb[:], in_=w_kv_down.rearrange("(p t) c -> p t c", t=PACK))
         wu_sb = const.tile([P, 2 * HEADS, R], BF16)
         x_sb = []
-        for s in range(STEPS):
-            x_step = x_pool.tile([P, TILES, C], BF16)
-            nc.sync.dma_start(
-                out=x_step[:],
-                in_=x_rows[s * STEP_TOKENS : (s + 1) * STEP_TOKENS, :].rearrange("(p n) c -> p n c", n=TILES),
-            )
-            x_sb.append(x_step)
-            if s == 0:
-                nc.sync.dma_start(out=wu_sb[:], in_=w_kv_up.rearrange("(b p) r -> p b r", p=P))
+        for s in range(N_PAIRS):
+            x_pair = x_pool.tile([P, PAIR, C], BF16)
+            x_sb.append(x_pair)
+        nc.sync.dma_start(out=wd_sb[:], in_=w_kv_down.rearrange("(p t) c -> p t c", t=PACK))
+        nc.sync.dma_start(out=x_sb[0][:], in_=x_rows[0])
+        nc.sync.dma_start(out=wu_sb[:], in_=w_kv_up.rearrange("(b p) r -> p b r", p=P))
+        for s in range(1, N_PAIRS):
+            nc.sync.dma_start(out=x_sb[s][:], in_=x_rows[s])
 
         cos_sb = const.tile([P, SEQ_TILES, HALF_D], BF16)
         sin_sb = const.tile([P, SEQ_TILES, HALF_D], BF16)
         gain_sb = const.tile([P, HALF_D, 2], BF16)
         nc.scalar.dma_start(
-            out=cos_sb[:].rearrange("p (s n) j -> p s n j", n=TILES),
-            in_=freqs_cos.rearrange("(s p n) j -> p s n j", p=P, n=TILES),
+            out=cos_sb[:].rearrange("p (s n) j -> p s n j", n=PAIR),
+            in_=freqs_cos.rearrange("(s p n) j -> p s n j", p=P, n=PAIR),
         )
         nc.scalar.dma_start(
-            out=sin_sb[:].rearrange("p (s n) j -> p s n j", n=TILES),
-            in_=freqs_sin.rearrange("(s p n) j -> p s n j", p=P, n=TILES),
+            out=sin_sb[:].rearrange("p (s n) j -> p s n j", n=PAIR),
+            in_=freqs_sin.rearrange("(s p n) j -> p s n j", p=P, n=PAIR),
         )
         nc.scalar.dma_start(out=gain_sb[:].rearrange("p j e -> p (j e)"), in_=k_norm_w.partition_broadcast(P))
 
@@ -96,165 +102,196 @@ def tile_mla_pa_t_kernel(
         table_warmer = const.tile([P, 1], F32)
         nc.scalar.activation(out=table_warmer[:], in_=eps[:], func=ACT.Sqrt)
 
-        partner_gain = const.tile([P, HALF_D, 2], F32)
-        nc.gpsimd.tensor_scalar_mul(out=partner_gain[:, :, 0], in0=gain_sb[:, :, 1], scalar1=-1.0)
-        nc.gpsimd.tensor_copy(out=partner_gain[:, :, 1], in_=gain_sb[:, :, 0])
-        own_table = const.tile([P, SEQ_TILES, HALF_D, 2], F32)
-        partner_table = const.tile([P, SEQ_TILES, HALF_D, 2], F32)
+        signed_gain = const.tile([P, HALF_D, 2], F32)
+        nc.gpsimd.tensor_copy(out=signed_gain[:, :, 0], in_=gain_sb[:, :, 0])
+        nc.gpsimd.tensor_scalar_mul(out=signed_gain[:, :, 1], in0=gain_sb[:, :, 1], scalar1=-1.0)
+        rope_table = const.tile([P, SEQ_TILES, 2, HALF_D, 2], F32)
         table_shape = [P, SEQ_TILES, HALF_D, 2]
         nc.gpsimd.tensor_tensor(
-            out=own_table[:],
+            out=rope_table[:, :, 0],
             in0=cos_sb[:].unsqueeze(3).to_broadcast(table_shape),
             in1=gain_sb[:].unsqueeze(1).to_broadcast(table_shape),
             op=ALU.mult,
         )
         nc.gpsimd.tensor_tensor(
-            out=partner_table[:],
+            out=rope_table[:, :, 1],
             in0=sin_sb[:].unsqueeze(3).to_broadcast(table_shape),
-            in1=partner_gain[:].unsqueeze(1).to_broadcast(table_shape),
+            in1=signed_gain[:].unsqueeze(1).to_broadcast(table_shape),
             op=ALU.mult,
         )
 
-        wd_grouped = const.tile([P, PACK * C_PASSES * P * PACK], BF16, align_bytes=64)
-        wd_codes = const.tile([P, PACK, C_PASSES, P], U32, align_bytes=64)
-        wd_scales = const.tile([P, PACK, C_PASSES, P], U8, align_bytes=64)
-        wd_grouped_twins = wd_grouped[:].bitcast(F32).rearrange("q (t g r u) -> q t g r u", t=PACK, g=C_PASSES, u=2)
-        for t in range(PACK):
-            twins_to_partitions(
-                nc, psum, identity[:], channel_blocks(wd_sb[:, t, :]), wd_grouped_twins[:, t], nc.vector.tensor_copy
-            )
-        nc.vector.quantize_mx(
-            out=wd_codes[:].rearrange("q t g r -> q (t g r)").bitcast(FP8X4),
-            scales=wd_scales[:].rearrange("q t g r -> q (t g r)"),
-            in_=wd_grouped[:],
-        )
+        def quantise_weight(block_sets, codes, scales, name):
+            for i in range(len(block_sets)):
+                bank = psum.tile([P, 2, 2, P], F32, tag="k", bufs=3)
+                transpose_twins(nc, bank, identity[:], block_sets[i])
+                grouped = const.tile([P, 2 * P * PACK], BF16, align_bytes=64, name="%s_grouped_%d" % (name, i))
+                group_twins(nc.vector.tensor_copy if i % 2 == 0 else nc.scalar.copy, bank, grouped)
+                columns = slice(2 * P * i, 2 * P * (i + 1))
+                nc.vector.quantize_mx(out=codes[:, columns].bitcast(FP8X4), scales=scales[:, columns], in_=grouped[:])
 
-        def quantise_w_kv_up():
-            grouped = const.tile([P, 2 * KEY_COLS * PACK], BF16, align_bytes=64, name="wu_grouped")
-            grouped_twins = grouped[:].bitcast(F32).rearrange("q (c a r u) -> q c a r u", a=2, r=P, u=2)
-            for c in range(HEADS):
-                blocks = [
-                    [wu_sb[:, 2 * c + a, :].bitcast(F32).rearrange("o (q u) -> o u q", u=2)[:, u, :] for u in range(2)]
-                    for a in range(2)
-                ]
-                twins_to_partitions(nc, psum, identity[:], blocks, grouped_twins[:, c], nc.vector.tensor_copy)
-            nc.vector.quantize_mx(out=wu_codes[:].bitcast(FP8X4), scales=wu_scales[:], in_=grouped[:])
-
+        wd_codes = const.tile([P, PACK * C_PASSES * P], U32, align_bytes=64)
+        wd_scales = const.tile([P, PACK * C_PASSES * P], U8, align_bytes=64)
         wu_codes = const.tile([P, 2 * KEY_COLS], U32, align_bytes=64)
         wu_scales = const.tile([P, 2 * KEY_COLS], U8, align_bytes=64)
 
-        def quantise_x(s):
-            grouped = step_pool.tile([P, TILES * C_PASSES * P * PACK], BF16, align_bytes=64, name="x_grouped")
-            codes = step_pool.tile([P, TILES, C_PASSES, P], U32, align_bytes=64, name="x_codes")
-            scales = step_pool.tile([P, TILES, C_PASSES, P], U8, align_bytes=64, name="x_scales")
-            grouped_twins = grouped[:].bitcast(F32).rearrange("q (n g r u) -> q n g r u", n=TILES, g=C_PASSES, u=2)
-            for n in range(TILES):
-                twins_to_partitions(
-                    nc, psum, identity[:], channel_blocks(x_sb[s][:, n, :]), grouped_twins[:, n], nc.scalar.copy
-                )
-            nc.vector.quantize_mx(
-                out=codes[:].rearrange("q n g r -> q (n g r)").bitcast(FP8X4),
-                scales=scales[:].rearrange("q n g r -> q (n g r)"),
-                in_=grouped[:],
-            )
-            return codes, scales
+        def every_second_twin(rows):
+            twins = rows.bitcast(F32).rearrange("o (q u) -> o u q", u=2)
+            return [twins[:, u, :] for u in range(2)]
 
-        def quantised_latent(x_codes, x_scales):
-            grouped = step_pool.tile([P, TILES, P, PACK], BF16, align_bytes=64, name="latent_grouped")
-            codes = step_pool.tile([P, TILES, P], U32, align_bytes=64, name="latent_codes")
-            scales = step_pool.tile([P, TILES, P], U8, align_bytes=64, name="latent_scales")
-            for n in range(TILES):
-                latent_ps = psum.tile([P, PACK, P], F32, tag="latent")
-                for t in range(PACK):
-                    for g in range(C_PASSES):
-                        nc.tensor.matmul_mx(
-                            out=latent_ps[:, t, :],
-                            lhsT=wd_codes[:, t, g, :].bitcast(FP8X4),
-                            lhsT_scale=wd_scales[:, t, g, :],
-                            rhs=x_codes[:, n, g, :].bitcast(FP8X4),
-                            rhs_scale=x_scales[:, n, g, :],
-                            start=(g == 0),
-                            stop=(g == C_PASSES - 1),
-                        )
-                nc.scalar.copy(out=grouped[:, n, :, :], in_=latent_ps[:].rearrange("p t r -> p r t"))
-            nc.vector.quantize_mx(
-                out=codes[:].rearrange("p n r -> p (n r)").bitcast(FP8X4),
-                scales=scales[:].rearrange("p n r -> p (n r)"),
-                in_=grouped[:].rearrange("p n r t -> p (n r t)"),
-            )
-            return codes, scales
+        twin_bank, x_codes, x_scales, x_grouped = {}, {}, {}, {}
+        latent_bank, latent_codes, latent_scales, latent_grouped = {}, {}, {}, {}
+        k_bank, v_bank, sum_squares, rms, rstd = {}, {}, {}, {}, {}
+        k_out, v_out = {}, {}
 
-        def keys_and_values(s, latent_codes, latent_scales):
-            k_out = step_pool.tile([P, TILES, KEY_COLS], F32)
-            v_out = step_pool.tile([P, TILES, KEY_COLS], F32)
-            for n in range(TILES):
-                k_ps = psum.tile([P, HEADS, HALF_D, 2], F32, tag="k")
-                v_ps = psum.tile([P, KEY_COLS], F32, tag="v")
-                for half_ps, first_col in ((k_ps[:].rearrange("p h j e -> p (h j e)"), 0), (v_ps[:], KEY_COLS)):
+        def transpose_x(k):
+            twin_bank[k] = psum.tile([P, 2, 2, P], F32, tag="twins", bufs=2, name="twin_bank")
+            transpose_twins(nc, twin_bank[k], identity[:], channel_blocks(x_sb[k // PAIR][:, k % PAIR, :]))
+
+        def group_x(k):
+            x_grouped[k] = work.tile([P, C_PASSES * P * PACK], BF16, align_bytes=64, name="x_grouped")
+            group_twins(nc.scalar.copy, twin_bank[k], x_grouped[k])
+
+        def quantise_x(k):
+            x_codes[k] = work.tile([P, C_PASSES, P], U32, align_bytes=64, name="x_codes")
+            x_scales[k] = work.tile([P, C_PASSES, P], U8, align_bytes=64, name="x_scales")
+            nc.vector.quantize_mx(
+                out=x_codes[k][:].rearrange("q g r -> q (g r)").bitcast(FP8X4),
+                scales=x_scales[k][:].rearrange("q g r -> q (g r)"),
+                in_=x_grouped[k][:],
+            )
+
+        def latent_passes(k):
+            latent_bank[k] = psum.tile([P, PACK, P], F32, tag="latent", bufs=1, name="latent_bank")
+            for t in range(PACK):
+                for g in range(C_PASSES):
+                    columns = slice((t * C_PASSES + g) * P, (t * C_PASSES + g + 1) * P)
                     nc.tensor.matmul_mx(
-                        out=half_ps,
-                        lhsT=latent_codes[:, n, :].bitcast(FP8X4),
-                        lhsT_scale=latent_scales[:, n, :],
-                        rhs=wu_codes[:, first_col : first_col + KEY_COLS].bitcast(FP8X4),
-                        rhs_scale=wu_scales[:, first_col : first_col + KEY_COLS],
-                        start=True,
-                        stop=True,
+                        out=latent_bank[k][:, t, :],
+                        lhsT=wd_codes[:, columns].bitcast(FP8X4),
+                        lhsT_scale=wd_scales[:, columns],
+                        rhs=x_codes[k][:, g, :].bitcast(FP8X4),
+                        rhs_scale=x_scales[k][:, g, :],
+                        start=(g == 0),
+                        stop=(g == C_PASSES - 1),
                     )
 
-                squares = tile_pool.tile([P, HEADS, HALF_D, 2], F32)
-                sum_squares = tile_pool.tile([P, HEADS], F32)
-                for h in range(HEADS):
-                    nc.scalar.activation(
-                        out=squares[:, h], in_=k_ps[:, h], func=ACT.Square, accum_out=sum_squares[:, h : h + 1]
-                    )
-                rms = tile_pool.tile([P, HEADS], F32)
-                nc.scalar.activation(out=rms[:], in_=sum_squares[:], func=ACT.Sqrt, scale=1.0 / D, bias=eps[:])
-                rstd = tile_pool.tile([P, HEADS], F32)
-                nc.vector.reciprocal(out=rstd[:], in_=rms[:])
+        def group_latent(k):
+            latent_grouped[k] = work.tile([P, P, PACK], BF16, align_bytes=64, name="latent_grouped")
+            nc.scalar.copy(out=latent_grouped[k][:], in_=latent_bank[k][:].rearrange("p t r -> p r t"))
 
-                if n % 2 == 0:
-                    nc.scalar.copy(out=v_out[:, n, :], in_=v_ps[:])
-                else:
-                    nc.vector.tensor_copy(out=v_out[:, n, :], in_=v_ps[:])
+        def quantise_latent(k):
+            latent_codes[k] = work.tile([P, P], U32, align_bytes=64, name="latent_codes")
+            latent_scales[k] = work.tile([P, P], U8, align_bytes=64, name="latent_scales")
+            nc.vector.quantize_mx(
+                out=latent_codes[k][:].bitcast(FP8X4),
+                scales=latent_scales[k][:],
+                in_=latent_grouped[k][:].rearrange("p r t -> p (r t)"),
+            )
 
-                position = (s * TILES + n) % SEQ_TILES
-                own = tile_pool.tile([P, HEADS, HALF_D, 2], F32)
-                partner = tile_pool.tile([P, HEADS, HALF_D, 2], F32)
-                for h in range(HEADS):
-                    nc.vector.scalar_tensor_tensor(
-                        out=own[:, h],
-                        in0=k_ps[:, h],
-                        scalar=rstd[:, h : h + 1],
-                        in1=own_table[:, position],
-                        op0=ALU.mult,
-                        op1=ALU.mult,
-                    )
-                    nc.vector.scalar_tensor_tensor(
-                        out=partner[:, h],
-                        in0=k_ps[:, h, :, ::-1],
-                        scalar=rstd[:, h : h + 1],
-                        in1=partner_table[:, position],
-                        op0=ALU.mult,
-                        op1=ALU.mult,
-                    )
-                nc.gpsimd.tensor_tensor(
-                    out=k_out[:, n, :],
-                    in0=own[:].rearrange("p h j e -> p (h j e)"),
-                    in1=partner[:].rearrange("p h j e -> p (h j e)"),
-                    op=ALU.add,
+        def kv_passes(k):
+            k_bank[k] = psum.tile([P, HEADS, D], F32, tag="k", bufs=3, name="k_bank")
+            v_bank[k] = psum.tile([P, KEY_COLS], F32, tag="v", bufs=2, name="v_bank")
+            for bank, first_col in ((k_bank[k][:].rearrange("p h d -> p (h d)"), 0), (v_bank[k][:], KEY_COLS)):
+                nc.tensor.matmul_mx(
+                    out=bank,
+                    lhsT=latent_codes[k][:].bitcast(FP8X4),
+                    lhsT_scale=latent_scales[k][:],
+                    rhs=wu_codes[:, first_col : first_col + KEY_COLS].bitcast(FP8X4),
+                    rhs_scale=wu_scales[:, first_col : first_col + KEY_COLS],
+                    start=True,
+                    stop=True,
                 )
-            step_rows = slice(s * STEP_TOKENS, (s + 1) * STEP_TOKENS)
-            nc.sync.dma_start(out=k_rows[step_rows, :].rearrange("(p n) f -> p n f", n=TILES), in_=k_out[:])
-            nc.sync.dma_start(out=v_rows[step_rows, :].rearrange("(p n) f -> p n f", n=TILES), in_=v_out[:])
 
-        x_quantised = {}
-        latent_quantised = {}
-        for i in range(STEPS + 2):
-            if i < STEPS:
-                x_quantised[i] = quantise_x(i)
-            if i == 0:
-                quantise_w_kv_up()
-            if 1 <= i <= STEPS:
-                latent_quantised[i - 1] = quantised_latent(*x_quantised[i - 1])
-            if i >= 2:
-                keys_and_values(i - 2, *latent_quantised[i - 2])
+        def sum_key_squares(k):
+            squares = work.tile([P, HEADS, D], F32)
+            sum_squares[k] = work.tile([P, HEADS], F32, name="sum_squares")
+            for h in range(HEADS):
+                nc.scalar.activation(
+                    out=squares[:, h], in_=k_bank[k][:, h], func=ACT.Square, accum_out=sum_squares[k][:, h : h + 1]
+                )
+
+        def root_mean_square(k):
+            rms[k] = work.tile([P, HEADS], F32, name="rms")
+            nc.scalar.activation(out=rms[k][:], in_=sum_squares[k][:], func=ACT.Sqrt, scale=1.0 / D, bias=eps[:])
+
+        def invert_rms(k):
+            rstd[k] = work.tile([P, HEADS], F32, name="rstd")
+            nc.vector.reciprocal(out=rstd[k][:], in_=rms[k][:])
+
+        def copy_values(k, copy_out):
+            if k % PAIR == 0:
+                v_out[k // PAIR] = work.tile([P, PAIR, KEY_COLS], F32, name="v_out")
+            copy_out(out=v_out[k // PAIR][:, k % PAIR, :], in_=v_bank[k][:])
+
+        def normalise_and_rotate(k):
+            if k % PAIR == 0:
+                k_out[k // PAIR] = work.tile([P, PAIR, KEY_COLS], F32, name="k_out")
+            products = work.tile([P, HEADS, 2, HALF_D, 2], F32)
+            for h in range(HEADS):
+                nc.vector.scalar_tensor_tensor(
+                    out=products[:, h].rearrange("p w j e -> p w (j e)"),
+                    in0=k_bank[k][:, h].unsqueeze(1).to_broadcast([P, 2, D]),
+                    scalar=rstd[k][:, h : h + 1],
+                    in1=rope_table[:, k % SEQ_TILES].rearrange("p w j e -> p w (j e)"),
+                    op0=ALU.mult,
+                    op1=ALU.mult,
+                )
+            nc.gpsimd.tensor_tensor(
+                out=k_out[k // PAIR][:, k % PAIR, :].rearrange("p (h j e) -> p h j e", h=HEADS, e=2),
+                in0=products[:, :, 0],
+                in1=products[:, :, 1, :, ::-1],
+                op=ALU.add,
+            )
+
+        def store_pair(s):
+            nc.sync.dma_start(out=k_rows[s], in_=k_out[s][:])
+            nc.sync.dma_start(out=v_rows[s], in_=v_out[s][:])
+
+        quantise_weight([channel_blocks(wd_sb[:, t, :]) for t in range(PACK)], wd_codes, wd_scales, "wd")
+        transpose_x(0)
+        transpose_x(1)
+        for k in range(N_TILES + FINISH_LAG):
+            mid = k - LATENT_LAG
+            last = k - FINISH_LAG
+            starts = k < N_TILES
+            has_mid = 0 <= mid < N_TILES
+            finishes = last >= 0
+
+            if finishes:
+                sum_key_squares(last)
+            if starts:
+                group_x(k)
+            if finishes:
+                root_mean_square(last)
+            if has_mid:
+                group_latent(mid)
+            if finishes and last % 2 == 1:
+                copy_values(last, nc.scalar.copy)
+
+            if finishes:
+                invert_rms(last)
+            if starts:
+                quantise_x(k)
+            if has_mid:
+                quantise_latent(mid)
+            if finishes and last % 2 == 0:
+                copy_values(last, nc.vector.tensor_copy)
+            if finishes:
+                normalise_and_rotate(last)
+                if last % PAIR == PAIR - 1:
+                    store_pair(last // PAIR)
+
+            if k % PAIR == 1 and k + PAIR < N_TILES:
+                transpose_x(k + 1)
+                transpose_x(k + 2)
+            if starts:
+                latent_passes(k)
+            if k == 0:
+                quantise_weight(
+                    [[every_second_twin(wu_sb[:, 2 * i + a, :]) for a in range(2)] for i in range(HEADS)],
+                    wu_codes,
+                    wu_scales,
+                    "wu",
+                )
+            if has_mid:
+                kv_passes(mid)

@@ -141,7 +141,7 @@ def tile_mla_pa_t_kernel(
         twin_bank, x_codes, x_scales, x_grouped = {}, {}, {}, {}
         latent_bank, latent_codes, latent_scales, latent_grouped = {}, {}, {}, {}
         k_bank, v_bank, sum_squares, rms, rstd = {}, {}, {}, {}, {}
-        k_out, v_out = {}, {}
+        k_out, v_out, products = {}, {}, {}
 
         def transpose_x(k):
             twin_bank[k] = psum.tile([P, 2, 2, P], F32, tag="twins", bufs=2, name="twin_bank")
@@ -224,22 +224,24 @@ def tile_mla_pa_t_kernel(
             copy_out(out=v_out[k // PAIR][:, k % PAIR, :], in_=v_bank[k][:])
 
         def normalise_and_rotate(k):
-            if k % PAIR == 0:
-                k_out[k // PAIR] = work.tile([P, PAIR, KEY_COLS], F32, name="k_out")
-            products = work.tile([P, HEADS, 2, HALF_D, 2], F32)
+            products[k] = work.tile([P, HEADS, 2, HALF_D, 2], F32, name="products")
             for h in range(HEADS):
                 nc.vector.scalar_tensor_tensor(
-                    out=products[:, h].rearrange("p w j e -> p w (j e)"),
+                    out=products[k][:, h].rearrange("p w j e -> p w (j e)"),
                     in0=k_bank[k][:, h].unsqueeze(1).to_broadcast([P, 2, D]),
                     scalar=rstd[k][:, h : h + 1],
                     in1=rope_table[:, k % SEQ_TILES].rearrange("p w j e -> p w (j e)"),
                     op0=ALU.mult,
                     op1=ALU.mult,
                 )
-            nc.gpsimd.tensor_tensor(
+
+        def sum_products(k):
+            if k % PAIR == 0:
+                k_out[k // PAIR] = work.tile([P, PAIR, KEY_COLS], F32, name="k_out")
+            nc.vector.tensor_tensor(
                 out=k_out[k // PAIR][:, k % PAIR, :].rearrange("p (h j e) -> p h j e", h=HEADS, e=2),
-                in0=products[:, :, 0],
-                in1=products[:, :, 1, :, ::-1],
+                in0=products[k][:, :, 0],
+                in1=products[k][:, :, 1, :, ::-1],
                 op=ALU.add,
             )
 
@@ -250,12 +252,13 @@ def tile_mla_pa_t_kernel(
         quantise_weight([channel_blocks(wd_sb[:, t, :]) for t in range(PACK)], wd_codes, wd_scales, "wd")
         transpose_x(0)
         transpose_x(1)
-        for k in range(N_TILES + FINISH_LAG):
+        for k in range(N_TILES + FINISH_LAG + 1):
             mid = k - LATENT_LAG
             last = k - FINISH_LAG
+            summed = last - 1
             starts = k < N_TILES
             has_mid = 0 <= mid < N_TILES
-            finishes = last >= 0
+            finishes = 0 <= last < N_TILES
 
             if finishes:
                 sum_key_squares(last)
@@ -265,7 +268,7 @@ def tile_mla_pa_t_kernel(
                 root_mean_square(last)
             if has_mid:
                 group_latent(mid)
-            if finishes and last % 2 == 1:
+            if finishes:
                 copy_values(last, nc.scalar.copy)
 
             if finishes:
@@ -274,12 +277,12 @@ def tile_mla_pa_t_kernel(
                 quantise_x(k)
             if has_mid:
                 quantise_latent(mid)
-            if finishes and last % 2 == 0:
-                copy_values(last, nc.vector.tensor_copy)
+            if summed >= 0:
+                sum_products(summed)
+                if summed % PAIR == PAIR - 1:
+                    store_pair(summed // PAIR)
             if finishes:
                 normalise_and_rotate(last)
-                if last % PAIR == PAIR - 1:
-                    store_pair(last // PAIR)
 
             if k % PAIR == 1 and k + PAIR < N_TILES:
                 transpose_x(k + 1)

@@ -30,29 +30,27 @@ N_TILES = TOKENS // P
 SEQ_TILES = SEQ // P
 PAIR = 2
 N_PAIRS = N_TILES // PAIR
-
-LATENT_LAG = 1
-FINISH_LAG = 3
+UNIT_COLS = PAIR * 2 * P
+WEIGHT_UNITS = 2
 
 FLOPS = 2 * TOKENS * C * R + 2 * TOKENS * R * 2 * KEY_COLS
 
 
-def transpose_twins(nc, bank, identity, twin_blocks):
-    for a in range(2):
-        for u in range(2):
-            nc.tensor.transpose(bank[:, a, u, :], twin_blocks[a][u], identity)
-
-
-def group_twins(copy_out, bank, grouped):
-    copy_out(
-        out=grouped[:].bitcast(F32).rearrange("q (a r u) -> q a r u", a=2, u=2),
-        in_=bank[:].rearrange("q a u r -> q a r u"),
-    )
+def block(i):
+    return slice(i * P, (i + 1) * P)
 
 
 def channel_blocks(rows):
     twins = rows.bitcast(F32)
-    return [[twins[:, (2 * g + u) * P : (2 * g + u + 1) * P] for u in range(2)] for g in range(C_PASSES)]
+    return [[twins[:, block(2 * g + u)] for u in range(2)] for g in range(C_PASSES)]
+
+
+def feature_blocks(rows_a, rows_b):
+    blocks = []
+    for rows in (rows_a, rows_b):
+        twins = rows.bitcast(F32).rearrange("o (q u) -> o u q", u=2)
+        blocks.append([twins[:, u, :] for u in range(2)])
+    return blocks
 
 
 def tile_mla_pa_t_kernel(
@@ -68,19 +66,16 @@ def tile_mla_pa_t_kernel(
         const = stack.enter_context(tc.tile_pool(name="const", bufs=1))
         x_pool = stack.enter_context(tc.tile_pool(name="x", bufs=N_PAIRS))
         work = stack.enter_context(tc.tile_pool(name="work", bufs=3))
-        psum = stack.enter_context(tc.psum_pool(name="psum", bufs=1))
 
         wd_sb = const.tile([P, PACK, C], BF16)
         wu_sb = const.tile([P, 2 * HEADS, R], BF16)
+        nc.sync.dma_start(out=wd_sb[:], in_=w_kv_down.rearrange("(p t) c -> p t c", t=PACK))
         x_sb = []
         for s in range(N_PAIRS):
             x_pair = x_pool.tile([P, PAIR, C], BF16)
+            nc.sync.dma_start(out=x_pair[:], in_=x_rows[s])
             x_sb.append(x_pair)
-        nc.sync.dma_start(out=wd_sb[:], in_=w_kv_down.rearrange("(p t) c -> p t c", t=PACK))
-        nc.sync.dma_start(out=x_sb[0][:], in_=x_rows[0])
         nc.sync.dma_start(out=wu_sb[:], in_=w_kv_up.rearrange("(b p) r -> p b r", p=P))
-        for s in range(1, N_PAIRS):
-            nc.sync.dma_start(out=x_sb[s][:], in_=x_rows[s])
 
         cos_sb = const.tile([P, SEQ_TILES, HALF_D], BF16)
         sin_sb = const.tile([P, SEQ_TILES, HALF_D], BF16)
@@ -103,198 +98,197 @@ def tile_mla_pa_t_kernel(
         nc.scalar.activation(out=table_warmer[:], in_=eps[:], func=ACT.Sqrt)
 
         signed_gain = const.tile([P, HALF_D, 2], F32)
-        nc.gpsimd.tensor_copy(out=signed_gain[:, :, 0], in_=gain_sb[:, :, 0])
-        nc.gpsimd.tensor_scalar_mul(out=signed_gain[:, :, 1], in0=gain_sb[:, :, 1], scalar1=-1.0)
+        nc.vector.tensor_copy(out=signed_gain[:, :, 0], in_=gain_sb[:, :, 0])
+        nc.vector.tensor_scalar_mul(out=signed_gain[:, :, 1], in0=gain_sb[:, :, 1], scalar1=-1.0)
         rope_table = const.tile([P, SEQ_TILES, 2, HALF_D, 2], F32)
         table_shape = [P, SEQ_TILES, HALF_D, 2]
-        nc.gpsimd.tensor_tensor(
+        nc.vector.tensor_tensor(
             out=rope_table[:, :, 0],
             in0=cos_sb[:].unsqueeze(3).to_broadcast(table_shape),
             in1=gain_sb[:].unsqueeze(1).to_broadcast(table_shape),
             op=ALU.mult,
         )
-        nc.gpsimd.tensor_tensor(
+        nc.vector.tensor_tensor(
             out=rope_table[:, :, 1],
             in0=sin_sb[:].unsqueeze(3).to_broadcast(table_shape),
             in1=signed_gain[:].unsqueeze(1).to_broadcast(table_shape),
             op=ALU.mult,
         )
 
-        def quantise_weight(block_sets, codes, scales, name):
-            for i in range(len(block_sets)):
-                bank = psum.tile([P, 2, 2, P], F32, tag="k", bufs=3)
-                transpose_twins(nc, bank, identity[:], block_sets[i])
-                grouped = const.tile([P, 2 * P * PACK], BF16, align_bytes=64, name="%s_grouped_%d" % (name, i))
-                group_twins(nc.vector.tensor_copy if i % 2 == 0 else nc.scalar.copy, bank, grouped)
-                columns = slice(2 * P * i, 2 * P * (i + 1))
-                nc.vector.quantize_mx(out=codes[:, columns].bitcast(FP8X4), scales=scales[:, columns], in_=grouped[:])
+        wd_codes = const.tile([P, WEIGHT_UNITS * UNIT_COLS], U32, align_bytes=64)
+        wd_scales = const.tile([P, WEIGHT_UNITS * UNIT_COLS], U8, align_bytes=64)
+        wu_codes = const.tile([P, WEIGHT_UNITS * UNIT_COLS], U32, align_bytes=64)
+        wu_scales = const.tile([P, WEIGHT_UNITS * UNIT_COLS], U8, align_bytes=64)
+        latent_codes = const.tile([P, N_TILES * P], U32, align_bytes=64)
+        latent_scales = const.tile([P, N_TILES * P], U8, align_bytes=64)
 
-        wd_codes = const.tile([P, PACK * C_PASSES * P], U32, align_bytes=64)
-        wd_scales = const.tile([P, PACK * C_PASSES * P], U8, align_bytes=64)
-        wu_codes = const.tile([P, 2 * KEY_COLS], U32, align_bytes=64)
-        wu_scales = const.tile([P, 2 * KEY_COLS], U8, align_bytes=64)
+        FIRST_X = WEIGHT_UNITS
+        FIRST_UP = FIRST_X + N_PAIRS
+        N_UNITS = FIRST_UP + WEIGHT_UNITS
 
-        def every_second_twin(rows):
-            twins = rows.bitcast(F32).rearrange("o (q u) -> o u q", u=2)
-            return [twins[:, u, :] for u in range(2)]
-
-        twin_bank, x_codes, x_scales, x_grouped = {}, {}, {}, {}
-        latent_bank, latent_codes, latent_scales, latent_grouped = {}, {}, {}, {}
-        k_bank, v_bank, sum_squares, rms, rstd = {}, {}, {}, {}, {}
-        k_out, v_out, products = {}, {}, {}
-
-        def transpose_x(k):
-            twin_bank[k] = psum.tile([P, 2, 2, P], F32, tag="twins", bufs=2, name="twin_bank")
-            transpose_twins(nc, twin_bank[k], identity[:], channel_blocks(x_sb[k // PAIR][:, k % PAIR, :]))
-
-        def group_x(k):
-            x_grouped[k] = work.tile([P, C_PASSES * P * PACK], BF16, align_bytes=64, name="x_grouped")
-            group_twins(nc.scalar.copy, twin_bank[k], x_grouped[k])
-
-        def quantise_x(k):
-            x_codes[k] = work.tile([P, C_PASSES, P], U32, align_bytes=64, name="x_codes")
-            x_scales[k] = work.tile([P, C_PASSES, P], U8, align_bytes=64, name="x_scales")
-            nc.vector.quantize_mx(
-                out=x_codes[k][:].rearrange("q g r -> q (g r)").bitcast(FP8X4),
-                scales=x_scales[k][:].rearrange("q g r -> q (g r)"),
-                in_=x_grouped[k][:],
+        unit_blocks = []
+        unit_codes = {}
+        for i in range(WEIGHT_UNITS):
+            unit_blocks.append([channel_blocks(wd_sb[:, PAIR * i + n, :]) for n in range(PAIR)])
+        for s in range(N_PAIRS):
+            unit_blocks.append([channel_blocks(x_sb[s][:, n, :]) for n in range(PAIR)])
+        for i in range(WEIGHT_UNITS):
+            unit_blocks.append(
+                [feature_blocks(wu_sb[:, 4 * i + 2 * n, :], wu_sb[:, 4 * i + 2 * n + 1, :]) for n in range(PAIR)]
             )
+        for i in range(WEIGHT_UNITS):
+            columns = slice(i * UNIT_COLS, (i + 1) * UNIT_COLS)
+            unit_codes[i] = (wd_codes[:, columns], wd_scales[:, columns])
+            unit_codes[FIRST_UP + i] = (wu_codes[:, columns], wu_scales[:, columns])
 
-        def latent_passes(k):
-            latent_bank[k] = psum.tile([P, PACK, P], F32, tag="latent", bufs=1, name="latent_bank")
-            for t in range(PACK):
-                for g in range(C_PASSES):
-                    columns = slice((t * C_PASSES + g) * P, (t * C_PASSES + g + 1) * P)
+        twin_banks, grouped, latent_banks, latent_grouped = {}, {}, {}, {}
+
+        with tc.psum_pool(name="phase1", bufs=4, reuse_waits="tile") as psum:
+
+            def transpose_unit(u):
+                twin_banks[u] = []
+                for n in range(PAIR):
+                    bank = psum.tile([P, 2, 2, P], F32, tag="twins")
+                    for a in range(2):
+                        for half in range(2):
+                            nc.tensor.transpose(bank[:, a, half, :], unit_blocks[u][n][a][half], identity[:])
+                    twin_banks[u].append(bank)
+
+            def group_unit(u):
+                grouped[u] = work.tile([P, UNIT_COLS * PACK], BF16, align_bytes=64, name="grouped")
+                words = grouped[u][:].bitcast(F32).rearrange("q (n a r u) -> q n a r u", n=PAIR, a=2, u=2)
+                nc.scalar.copy(out=words[:, 0], in_=twin_banks[u][0][:].rearrange("q a u r -> q a r u"))
+                nc.vector.tensor_copy(out=words[:, 1], in_=twin_banks[u][1][:].rearrange("q a u r -> q a r u"))
+
+            def quantise_unit(u):
+                if u not in unit_codes:
+                    x_codes = work.tile([P, UNIT_COLS], U32, align_bytes=64)
+                    x_scales = work.tile([P, UNIT_COLS], U8, align_bytes=64)
+                    unit_codes[u] = (x_codes[:], x_scales[:])
+                codes, scales = unit_codes[u]
+                nc.vector.quantize_mx(out=codes.bitcast(FP8X4), scales=scales, in_=grouped[u][:])
+
+            def latent_passes(s):
+                x_codes, x_scales = unit_codes[FIRST_X + s]
+                latent_banks[s] = []
+                for n in range(PAIR):
+                    bank = psum.tile([P, PACK, P], F32, tag="latent")
+                    for t in range(PACK):
+                        for g in range(C_PASSES):
+                            nc.tensor.matmul_mx(
+                                out=bank[:, t, :],
+                                lhsT=wd_codes[:, block(t * C_PASSES + g)].bitcast(FP8X4),
+                                lhsT_scale=wd_scales[:, block(t * C_PASSES + g)],
+                                rhs=x_codes[:, block(n * C_PASSES + g)].bitcast(FP8X4),
+                                rhs_scale=x_scales[:, block(n * C_PASSES + g)],
+                                start=(g == 0),
+                                stop=(g == C_PASSES - 1),
+                            )
+                    latent_banks[s].append(bank)
+
+            def group_latent(s):
+                latent_grouped[s] = work.tile([P, PAIR, P, PACK], BF16, align_bytes=64, name="latent_grouped")
+                for n in range(PAIR):
+                    nc.scalar.copy(out=latent_grouped[s][:, n], in_=latent_banks[s][n][:].rearrange("p t r -> p r t"))
+
+            def quantise_latent(s):
+                columns = slice(s * PAIR * P, (s + 1) * PAIR * P)
+                nc.vector.quantize_mx(
+                    out=latent_codes[:, columns].bitcast(FP8X4),
+                    scales=latent_scales[:, columns],
+                    in_=latent_grouped[s][:].rearrange("p n r t -> p (n r t)"),
+                )
+
+            for j in range(N_UNITS + 3):
+                if j < N_UNITS:
+                    transpose_unit(j)
+                if 0 <= j - 1 < N_UNITS:
+                    group_unit(j - 1)
+                if 0 <= j - 2 < N_UNITS:
+                    quantise_unit(j - 2)
+                s = j - 3 - FIRST_X
+                if 0 <= s < N_PAIRS:
+                    latent_passes(s)
+                if 0 <= s - 1 < N_PAIRS:
+                    group_latent(s - 1)
+                if 0 <= s - 2 < N_PAIRS:
+                    quantise_latent(s - 2)
+
+        k_banks, v_banks, sum_squares, rms, rstd, products, k_out, v_out = {}, {}, {}, {}, {}, {}, {}, {}
+
+        with tc.psum_pool(name="phase2", bufs=1, reuse_waits="tile") as psum:
+
+            def kv_passes(k):
+                k_banks[k] = psum.tile([P, HEADS, D], F32, tag="k", bufs=5, name="k_bank")
+                v_banks[k] = psum.tile([P, KEY_COLS], F32, tag="v", bufs=3, name="v_bank")
+                for bank, first_col in ((k_banks[k][:].rearrange("p h d -> p (h d)"), 0), (v_banks[k][:], KEY_COLS)):
                     nc.tensor.matmul_mx(
-                        out=latent_bank[k][:, t, :],
-                        lhsT=wd_codes[:, columns].bitcast(FP8X4),
-                        lhsT_scale=wd_scales[:, columns],
-                        rhs=x_codes[k][:, g, :].bitcast(FP8X4),
-                        rhs_scale=x_scales[k][:, g, :],
-                        start=(g == 0),
-                        stop=(g == C_PASSES - 1),
+                        out=bank,
+                        lhsT=latent_codes[:, block(k)].bitcast(FP8X4),
+                        lhsT_scale=latent_scales[:, block(k)],
+                        rhs=wu_codes[:, first_col : first_col + KEY_COLS].bitcast(FP8X4),
+                        rhs_scale=wu_scales[:, first_col : first_col + KEY_COLS],
+                        start=True,
+                        stop=True,
                     )
 
-        def group_latent(k):
-            latent_grouped[k] = work.tile([P, P, PACK], BF16, align_bytes=64, name="latent_grouped")
-            nc.scalar.copy(out=latent_grouped[k][:], in_=latent_bank[k][:].rearrange("p t r -> p r t"))
+            def sum_key_squares(k):
+                squares = work.tile([P, HEADS, D], F32)
+                sum_squares[k] = work.tile([P, HEADS], F32, name="sum_squares")
+                for h in range(HEADS):
+                    nc.scalar.activation(
+                        out=squares[:, h], in_=k_banks[k][:, h], func=ACT.Square, accum_out=sum_squares[k][:, h : h + 1]
+                    )
 
-        def quantise_latent(k):
-            latent_codes[k] = work.tile([P, P], U32, align_bytes=64, name="latent_codes")
-            latent_scales[k] = work.tile([P, P], U8, align_bytes=64, name="latent_scales")
-            nc.vector.quantize_mx(
-                out=latent_codes[k][:].bitcast(FP8X4),
-                scales=latent_scales[k][:],
-                in_=latent_grouped[k][:].rearrange("p r t -> p (r t)"),
-            )
+            def copy_values(k):
+                if k % PAIR == 0:
+                    v_out[k // PAIR] = work.tile([P, PAIR, KEY_COLS], F32, name="v_out")
+                nc.scalar.copy(out=v_out[k // PAIR][:, k % PAIR, :], in_=v_banks[k][:])
+                if k % PAIR == PAIR - 1:
+                    nc.sync.dma_start(out=v_rows[k // PAIR], in_=v_out[k // PAIR][:])
 
-        def kv_passes(k):
-            k_bank[k] = psum.tile([P, HEADS, D], F32, tag="k", bufs=3, name="k_bank")
-            v_bank[k] = psum.tile([P, KEY_COLS], F32, tag="v", bufs=2, name="v_bank")
-            for bank, first_col in ((k_bank[k][:].rearrange("p h d -> p (h d)"), 0), (v_bank[k][:], KEY_COLS)):
-                nc.tensor.matmul_mx(
-                    out=bank,
-                    lhsT=latent_codes[k][:].bitcast(FP8X4),
-                    lhsT_scale=latent_scales[k][:],
-                    rhs=wu_codes[:, first_col : first_col + KEY_COLS].bitcast(FP8X4),
-                    rhs_scale=wu_scales[:, first_col : first_col + KEY_COLS],
-                    start=True,
-                    stop=True,
+            def root_mean_square(k):
+                rms[k] = work.tile([P, HEADS], F32, name="rms")
+                nc.scalar.activation(out=rms[k][:], in_=sum_squares[k][:], func=ACT.Sqrt, scale=1.0 / D, bias=eps[:])
+
+            def invert_rms(k):
+                rstd[k] = work.tile([P, HEADS], F32, name="rstd")
+                nc.vector.reciprocal(out=rstd[k][:], in_=rms[k][:])
+
+            def multiply_keys(k):
+                products[k] = work.tile([P, HEADS, 2, HALF_D, 2], F32, name="products", bufs=4)
+                for h in range(HEADS):
+                    nc.vector.scalar_tensor_tensor(
+                        out=products[k][:, h].rearrange("p w j e -> p w (j e)"),
+                        in0=k_banks[k][:, h].unsqueeze(1).to_broadcast([P, 2, D]),
+                        scalar=rstd[k][:, h : h + 1],
+                        in1=rope_table[:, k % SEQ_TILES].rearrange("p w j e -> p w (j e)"),
+                        op0=ALU.mult,
+                        op1=ALU.mult,
+                    )
+
+            def sum_products(k):
+                if k % PAIR == 0:
+                    k_out[k // PAIR] = work.tile([P, PAIR, KEY_COLS], F32, name="k_out")
+                nc.gpsimd.tensor_tensor(
+                    out=k_out[k // PAIR][:, k % PAIR, :].rearrange("p (h j e) -> p h j e", h=HEADS, e=2),
+                    in0=products[k][:, :, 0],
+                    in1=products[k][:, :, 1, :, ::-1],
+                    op=ALU.add,
                 )
+                if k % PAIR == PAIR - 1:
+                    nc.sync.dma_start(out=k_rows[k // PAIR], in_=k_out[k // PAIR][:])
 
-        def sum_key_squares(k):
-            squares = work.tile([P, HEADS, D], F32)
-            sum_squares[k] = work.tile([P, HEADS], F32, name="sum_squares")
-            for h in range(HEADS):
-                nc.scalar.activation(
-                    out=squares[:, h], in_=k_bank[k][:, h], func=ACT.Square, accum_out=sum_squares[k][:, h : h + 1]
-                )
-
-        def root_mean_square(k):
-            rms[k] = work.tile([P, HEADS], F32, name="rms")
-            nc.scalar.activation(out=rms[k][:], in_=sum_squares[k][:], func=ACT.Sqrt, scale=1.0 / D, bias=eps[:])
-
-        def invert_rms(k):
-            rstd[k] = work.tile([P, HEADS], F32, name="rstd")
-            nc.vector.reciprocal(out=rstd[k][:], in_=rms[k][:])
-
-        def copy_values(k, copy_out):
-            if k % PAIR == 0:
-                v_out[k // PAIR] = work.tile([P, PAIR, KEY_COLS], F32, name="v_out")
-            copy_out(out=v_out[k // PAIR][:, k % PAIR, :], in_=v_bank[k][:])
-
-        def normalise_and_rotate(k):
-            products[k] = work.tile([P, HEADS, 2, HALF_D, 2], F32, name="products")
-            for h in range(HEADS):
-                nc.vector.scalar_tensor_tensor(
-                    out=products[k][:, h].rearrange("p w j e -> p w (j e)"),
-                    in0=k_bank[k][:, h].unsqueeze(1).to_broadcast([P, 2, D]),
-                    scalar=rstd[k][:, h : h + 1],
-                    in1=rope_table[:, k % SEQ_TILES].rearrange("p w j e -> p w (j e)"),
-                    op0=ALU.mult,
-                    op1=ALU.mult,
-                )
-
-        def sum_products(k):
-            if k % PAIR == 0:
-                k_out[k // PAIR] = work.tile([P, PAIR, KEY_COLS], F32, name="k_out")
-            nc.vector.tensor_tensor(
-                out=k_out[k // PAIR][:, k % PAIR, :].rearrange("p (h j e) -> p h j e", h=HEADS, e=2),
-                in0=products[k][:, :, 0],
-                in1=products[k][:, :, 1, :, ::-1],
-                op=ALU.add,
-            )
-
-        def store_pair(s):
-            nc.sync.dma_start(out=k_rows[s], in_=k_out[s][:])
-            nc.sync.dma_start(out=v_rows[s], in_=v_out[s][:])
-
-        quantise_weight([channel_blocks(wd_sb[:, t, :]) for t in range(PACK)], wd_codes, wd_scales, "wd")
-        transpose_x(0)
-        transpose_x(1)
-        for k in range(N_TILES + FINISH_LAG + 1):
-            mid = k - LATENT_LAG
-            last = k - FINISH_LAG
-            summed = last - 1
-            starts = k < N_TILES
-            has_mid = 0 <= mid < N_TILES
-            finishes = 0 <= last < N_TILES
-
-            if finishes:
-                sum_key_squares(last)
-            if starts:
-                group_x(k)
-            if finishes:
-                root_mean_square(last)
-            if has_mid:
-                group_latent(mid)
-            if finishes:
-                copy_values(last, nc.scalar.copy)
-
-            if finishes:
-                invert_rms(last)
-            if starts:
-                quantise_x(k)
-            if has_mid:
-                quantise_latent(mid)
-            if summed >= 0:
-                sum_products(summed)
-                if summed % PAIR == PAIR - 1:
-                    store_pair(summed // PAIR)
-            if finishes:
-                normalise_and_rotate(last)
-
-            if k % PAIR == 1 and k + PAIR < N_TILES:
-                transpose_x(k + 1)
-                transpose_x(k + 2)
-            if starts:
-                latent_passes(k)
-            if k == 0:
-                quantise_weight(
-                    [[every_second_twin(wu_sb[:, 2 * i + a, :]) for a in range(2)] for i in range(HEADS)],
-                    wu_codes,
-                    wu_scales,
-                    "wu",
-                )
-            if has_mid:
-                kv_passes(mid)
+            for j in range(N_TILES + 4):
+                if j < N_TILES:
+                    kv_passes(j)
+                if 0 <= j - 1 < N_TILES:
+                    sum_key_squares(j - 1)
+                    copy_values(j - 1)
+                    root_mean_square(j - 1)
+                if 0 <= j - 2 < N_TILES:
+                    invert_rms(j - 2)
+                if 0 <= j - 3 < N_TILES:
+                    multiply_keys(j - 3)
+                if 0 <= j - 4:
+                    sum_products(j - 4)

@@ -69,7 +69,9 @@ def tile_mla_pa_t_kernel(
 
         wd_sb = const.tile([P, PACK, C], BF16)
         wu_sb = const.tile([P, 2 * HEADS, R], BF16)
-        nc.sync.dma_start(out=wd_sb[:], in_=w_kv_down.rearrange("(p t) c -> p t c", t=PACK))
+        for i in range(WEIGHT_UNITS):
+            rows = slice(PAIR * i, PAIR * (i + 1))
+            nc.sync.dma_start(out=wd_sb[:, rows, :], in_=w_kv_down.rearrange("(p t) c -> p t c", t=PACK)[:, rows, :])
         x_sb = []
         for s in range(N_PAIRS):
             x_pair = x_pool.tile([P, PAIR, C], BF16)
@@ -95,7 +97,7 @@ def tile_mla_pa_t_kernel(
         eps = const.tile([P, 1], F32)
         nc.vector.memset(eps[:], EPS)
         table_warmer = const.tile([P, 1], F32)
-        nc.scalar.activation(out=table_warmer[:], in_=eps[:], func=ACT.Sqrt)
+        nc.scalar.activation(out=table_warmer[:], in_=eps[:], func=ACT.Abs_reciprocal_sqrt)
 
         signed_gain = const.tile([P, HALF_D, 2], F32)
         nc.vector.tensor_copy(out=signed_gain[:, :, 0], in_=gain_sb[:, :, 0])
@@ -214,7 +216,7 @@ def tile_mla_pa_t_kernel(
                 if 0 <= s - 2 < N_PAIRS:
                     quantise_latent(s - 2)
 
-        k_banks, v_banks, sum_squares, rms, rstd, products, k_out, v_out = {}, {}, {}, {}, {}, {}, {}, {}
+        k_banks, v_banks, sum_squares, rstd, products, k_out, v_out = {}, {}, {}, {}, {}, {}, {}
 
         with tc.psum_pool(name="phase2", bufs=1, reuse_waits="tile") as psum:
 
@@ -247,13 +249,11 @@ def tile_mla_pa_t_kernel(
                 if k % PAIR == PAIR - 1:
                     nc.sync.dma_start(out=v_rows[k // PAIR], in_=v_out[k // PAIR][:])
 
-            def root_mean_square(k):
-                rms[k] = work.tile([P, HEADS], F32, name="rms")
-                nc.scalar.activation(out=rms[k][:], in_=sum_squares[k][:], func=ACT.Sqrt, scale=1.0 / D, bias=eps[:])
-
-            def invert_rms(k):
+            def reciprocal_rms(k):
                 rstd[k] = work.tile([P, HEADS], F32, name="rstd")
-                nc.vector.reciprocal(out=rstd[k][:], in_=rms[k][:])
+                nc.scalar.activation(
+                    out=rstd[k][:], in_=sum_squares[k][:], func=ACT.Abs_reciprocal_sqrt, scale=1.0 / D, bias=eps[:]
+                )
 
             def multiply_keys(k):
                 products[k] = work.tile([P, HEADS, 2, HALF_D, 2], F32, name="products", bufs=4)
@@ -279,16 +279,14 @@ def tile_mla_pa_t_kernel(
                 if k % PAIR == PAIR - 1:
                     nc.sync.dma_start(out=k_rows[k // PAIR], in_=k_out[k // PAIR][:])
 
-            for j in range(N_TILES + 4):
+            for j in range(N_TILES + 3):
                 if j < N_TILES:
                     kv_passes(j)
                 if 0 <= j - 1 < N_TILES:
                     sum_key_squares(j - 1)
                     copy_values(j - 1)
-                    root_mean_square(j - 1)
+                    reciprocal_rms(j - 1)
                 if 0 <= j - 2 < N_TILES:
-                    invert_rms(j - 2)
-                if 0 <= j - 3 < N_TILES:
-                    multiply_keys(j - 3)
-                if 0 <= j - 4:
-                    sum_products(j - 4)
+                    multiply_keys(j - 2)
+                if 0 <= j - 3:
+                    sum_products(j - 3)

@@ -121,29 +121,28 @@ def tile_mla_pa_t_kernel(
         wd_scales = const.tile([P, WEIGHT_UNITS * UNIT_COLS], U8, align_bytes=64)
         wu_codes = const.tile([P, WEIGHT_UNITS * UNIT_COLS], U32, align_bytes=64)
         wu_scales = const.tile([P, WEIGHT_UNITS * UNIT_COLS], U8, align_bytes=64)
-        latent_codes = const.tile([P, N_TILES * P], U32, align_bytes=64)
-        latent_scales = const.tile([P, N_TILES * P], U8, align_bytes=64)
-
-        FIRST_X = WEIGHT_UNITS
-        FIRST_UP = FIRST_X + N_PAIRS
-        N_UNITS = FIRST_UP + WEIGHT_UNITS
+        x_codes = const.tile([P, N_PAIRS * UNIT_COLS], U32, align_bytes=64)
+        x_scales = const.tile([P, N_PAIRS * UNIT_COLS], U8, align_bytes=64)
 
         unit_blocks = []
-        unit_codes = {}
+        unit_codes = []
         for i in range(WEIGHT_UNITS):
+            columns = slice(i * UNIT_COLS, (i + 1) * UNIT_COLS)
             unit_blocks.append([channel_blocks(wd_sb[:, PAIR * i + n, :]) for n in range(PAIR)])
+            unit_codes.append((wd_codes[:, columns], wd_scales[:, columns]))
         for s in range(N_PAIRS):
+            columns = slice(s * UNIT_COLS, (s + 1) * UNIT_COLS)
             unit_blocks.append([channel_blocks(x_sb[s][:, n, :]) for n in range(PAIR)])
+            unit_codes.append((x_codes[:, columns], x_scales[:, columns]))
         for i in range(WEIGHT_UNITS):
+            columns = slice(i * UNIT_COLS, (i + 1) * UNIT_COLS)
             unit_blocks.append(
                 [feature_blocks(wu_sb[:, 4 * i + 2 * n, :], wu_sb[:, 4 * i + 2 * n + 1, :]) for n in range(PAIR)]
             )
-        for i in range(WEIGHT_UNITS):
-            columns = slice(i * UNIT_COLS, (i + 1) * UNIT_COLS)
-            unit_codes[i] = (wd_codes[:, columns], wd_scales[:, columns])
-            unit_codes[FIRST_UP + i] = (wu_codes[:, columns], wu_scales[:, columns])
+            unit_codes.append((wu_codes[:, columns], wu_scales[:, columns]))
+        n_units = len(unit_blocks)
 
-        twin_banks, grouped, latent_banks, latent_grouped = {}, {}, {}, {}
+        twin_banks, grouped = {}, {}
 
         with tc.psum_pool(name="phase1", bufs=4, reuse_waits="tile") as psum:
 
@@ -163,71 +162,58 @@ def tile_mla_pa_t_kernel(
                 nc.vector.tensor_copy(out=words[:, 1], in_=twin_banks[u][1][:].rearrange("q a u r -> q a r u"))
 
             def quantise_unit(u):
-                if u not in unit_codes:
-                    x_codes = work.tile([P, UNIT_COLS], U32, align_bytes=64)
-                    x_scales = work.tile([P, UNIT_COLS], U8, align_bytes=64)
-                    unit_codes[u] = (x_codes[:], x_scales[:])
                 codes, scales = unit_codes[u]
                 nc.vector.quantize_mx(out=codes.bitcast(FP8X4), scales=scales, in_=grouped[u][:])
 
-            def latent_passes(s):
-                x_codes, x_scales = unit_codes[FIRST_X + s]
-                latent_banks[s] = []
-                for n in range(PAIR):
-                    bank = psum.tile([P, PACK, P], F32, tag="latent")
-                    for t in range(PACK):
-                        for g in range(C_PASSES):
-                            nc.tensor.matmul_mx(
-                                out=bank[:, t, :],
-                                lhsT=wd_codes[:, block(t * C_PASSES + g)].bitcast(FP8X4),
-                                lhsT_scale=wd_scales[:, block(t * C_PASSES + g)],
-                                rhs=x_codes[:, block(n * C_PASSES + g)].bitcast(FP8X4),
-                                rhs_scale=x_scales[:, block(n * C_PASSES + g)],
-                                start=(g == 0),
-                                stop=(g == C_PASSES - 1),
-                            )
-                    latent_banks[s].append(bank)
-
-            def group_latent(s):
-                latent_grouped[s] = work.tile([P, PAIR, P, PACK], BF16, align_bytes=64, name="latent_grouped")
-                for n in range(PAIR):
-                    nc.scalar.copy(out=latent_grouped[s][:, n], in_=latent_banks[s][n][:].rearrange("p t r -> p r t"))
-
-            def quantise_latent(s):
-                columns = slice(s * PAIR * P, (s + 1) * PAIR * P)
-                nc.vector.quantize_mx(
-                    out=latent_codes[:, columns].bitcast(FP8X4),
-                    scales=latent_scales[:, columns],
-                    in_=latent_grouped[s][:].rearrange("p n r t -> p (n r t)"),
-                )
-
-            for j in range(N_UNITS + 3):
-                if j < N_UNITS:
+            for j in range(n_units + 2):
+                if j < n_units:
                     transpose_unit(j)
-                if 0 <= j - 1 < N_UNITS:
+                if 0 <= j - 1 < n_units:
                     group_unit(j - 1)
-                if 0 <= j - 2 < N_UNITS:
+                if 0 <= j - 2:
                     quantise_unit(j - 2)
-                s = j - 3 - FIRST_X
-                if 0 <= s < N_PAIRS:
-                    latent_passes(s)
-                if 0 <= s - 1 < N_PAIRS:
-                    group_latent(s - 1)
-                if 0 <= s - 2 < N_PAIRS:
-                    quantise_latent(s - 2)
 
+        latent_banks, latent_grouped, latent_codes = {}, {}, {}
         k_banks, v_banks, sum_squares, rstd, products, k_out, v_out = {}, {}, {}, {}, {}, {}, {}
 
-        with tc.psum_pool(name="phase2", bufs=1, reuse_waits="tile") as psum:
+        with tc.psum_pool(name="phase2", bufs=2, reuse_waits="tile") as psum:
+
+            def latent_passes(k):
+                latent_banks[k] = psum.tile([P, PACK, P], F32, tag="latent", name="latent_bank")
+                for t in range(PACK):
+                    for g in range(C_PASSES):
+                        nc.tensor.matmul_mx(
+                            out=latent_banks[k][:, t, :],
+                            lhsT=wd_codes[:, block(t * C_PASSES + g)].bitcast(FP8X4),
+                            lhsT_scale=wd_scales[:, block(t * C_PASSES + g)],
+                            rhs=x_codes[:, block(k * C_PASSES + g)].bitcast(FP8X4),
+                            rhs_scale=x_scales[:, block(k * C_PASSES + g)],
+                            start=(g == 0),
+                            stop=(g == C_PASSES - 1),
+                        )
+
+            def group_latent(k, copy_out):
+                if k % PAIR == 0:
+                    latent_grouped[k // PAIR] = work.tile([P, PAIR, P, PACK], BF16, align_bytes=64, name="latent_grouped")
+                copy_out(out=latent_grouped[k // PAIR][:, k % PAIR], in_=latent_banks[k][:].rearrange("p t r -> p r t"))
+
+            def quantise_latent(s):
+                codes = work.tile([P, PAIR * P], U32, align_bytes=64, name="latent_codes")
+                scales = work.tile([P, PAIR * P], U8, align_bytes=64, name="latent_scales")
+                nc.vector.quantize_mx(
+                    out=codes[:].bitcast(FP8X4), scales=scales[:], in_=latent_grouped[s][:].rearrange("p n r t -> p (n r t)")
+                )
+                latent_codes[s] = (codes, scales)
 
             def kv_passes(k):
-                k_banks[k] = psum.tile([P, HEADS, D], F32, tag="k", bufs=5, name="k_bank")
-                v_banks[k] = psum.tile([P, KEY_COLS], F32, tag="v", bufs=3, name="v_bank")
+                codes, scales = latent_codes[k // PAIR]
+                k_banks[k] = psum.tile([P, HEADS, D], F32, tag="k", bufs=4, name="k_bank")
+                v_banks[k] = psum.tile([P, KEY_COLS], F32, tag="v", name="v_bank")
                 for bank, first_col in ((k_banks[k][:].rearrange("p h d -> p (h d)"), 0), (v_banks[k][:], KEY_COLS)):
                     nc.tensor.matmul_mx(
                         out=bank,
-                        lhsT=latent_codes[:, block(k)].bitcast(FP8X4),
-                        lhsT_scale=latent_scales[:, block(k)],
+                        lhsT=codes[:, block(k % PAIR)].bitcast(FP8X4),
+                        lhsT_scale=scales[:, block(k % PAIR)],
                         rhs=wu_codes[:, first_col : first_col + KEY_COLS].bitcast(FP8X4),
                         rhs_scale=wu_scales[:, first_col : first_col + KEY_COLS],
                         start=True,
@@ -255,9 +241,10 @@ def tile_mla_pa_t_kernel(
                     out=rstd[k][:], in_=sum_squares[k][:], func=ACT.Abs_reciprocal_sqrt, scale=1.0 / D, bias=eps[:]
                 )
 
-            def multiply_keys(k):
-                products[k] = work.tile([P, HEADS, 2, HALF_D, 2], F32, name="products", bufs=4)
-                for h in range(HEADS):
+            def multiply_keys(k, heads):
+                if k not in products:
+                    products[k] = work.tile([P, HEADS, 2, HALF_D, 2], F32, name="products", bufs=4)
+                for h in heads:
                     nc.vector.scalar_tensor_tensor(
                         out=products[k][:, h].rearrange("p w j e -> p w (j e)"),
                         in0=k_banks[k][:, h].unsqueeze(1).to_broadcast([P, 2, D]),
@@ -279,14 +266,28 @@ def tile_mla_pa_t_kernel(
                 if k % PAIR == PAIR - 1:
                     nc.sync.dma_start(out=k_rows[k // PAIR], in_=k_out[k // PAIR][:])
 
-            for j in range(N_TILES + 3):
+            for j in range(N_TILES + 5):
+                grouping = j - 1
+                finishing = j - 4
+                multiplying = j - 5
+                vector_groups = 0 <= grouping < N_TILES and grouping % PAIR == PAIR - 1
+
                 if j < N_TILES:
-                    kv_passes(j)
-                if 0 <= j - 1 < N_TILES:
-                    sum_key_squares(j - 1)
-                    copy_values(j - 1)
-                    reciprocal_rms(j - 1)
-                if 0 <= j - 2 < N_TILES:
-                    multiply_keys(j - 2)
-                if 0 <= j - 3:
-                    sum_products(j - 3)
+                    latent_passes(j)
+                if 0 <= j - 3 < N_TILES:
+                    kv_passes(j - 3)
+                if 0 <= grouping < N_TILES and not vector_groups:
+                    group_latent(grouping, nc.scalar.copy)
+                if 0 <= finishing < N_TILES:
+                    sum_key_squares(finishing)
+                    copy_values(finishing)
+                    reciprocal_rms(finishing)
+                if vector_groups:
+                    group_latent(grouping, nc.vector.tensor_copy)
+                if 0 <= multiplying:
+                    multiply_keys(multiplying, range(HEADS - 1))
+                if vector_groups:
+                    quantise_latent(grouping // PAIR)
+                if 0 <= multiplying:
+                    multiply_keys(multiplying, range(HEADS - 1, HEADS))
+                    sum_products(multiplying)

from contextlib import ExitStack

import concourse.mybir as mybir
from concourse.masks import make_identity

F32 = mybir.dt.float32
BF16 = mybir.dt.bfloat16
U32 = mybir.dt.uint32
U8 = mybir.dt.uint8
FP8X4 = mybir.dt.float8_e4m3fn_x4
ALU = mybir.AluOpType
ACT = mybir.ActivationFunctionType

P = 128
PACK = 4
K_PASS = P * PACK

TOKENS = 4 * 1024
SEQ = 1024
C = 1024
R = 512
HEADS = 4
D = 128
HALF_D = D // 2
KEY_COLS = HEADS * D
EPS = 1e-6

C_PASSES = C // K_PASS
N_TILES = TOKENS // P
SEQ_TILES = SEQ // P
PAIR = 2
N_PAIRS = N_TILES // PAIR
UNIT_COLS = PAIR * 2 * P
WEIGHT_UNITS = 2

FLOPS = 2 * TOKENS * C * R + 2 * TOKENS * R * 2 * KEY_COLS


def block(i):
    return slice(i * P, (i + 1) * P)


def channel_blocks(rows):
    twins = rows.bitcast(F32)
    return [[twins[:, block(2 * g + u)] for u in range(2)] for g in range(C_PASSES)]


def feature_blocks(rows_a, rows_b):
    blocks = []
    for rows in (rows_a, rows_b):
        twins = rows.bitcast(F32).rearrange("o (q u) -> o u q", u=2)
        blocks.append([twins[:, u, :] for u in range(2)])
    return blocks


def tile_mla_pa_t_kernel(
    tc, x, w_kv_down, w_kv_up, k_norm_w, freqs_cos, freqs_sin, out_0, out_1
):
    nc = tc.nc
    x_rows = x.flatten_outer_dims().rearrange("(s p n) c -> s p n c", p=P, n=PAIR)
    k_rows = out_0.rearrange("b t h d -> (b t) (h d)").rearrange("(s p n) f -> s p n f", p=P, n=PAIR)
    v_rows = out_1.rearrange("b t h d -> (b t) (h d)").rearrange("(s p n) f -> s p n f", p=P, n=PAIR)

    with ExitStack() as stack:
        stack.enter_context(tc.manual_schedule())
        const = stack.enter_context(tc.tile_pool(name="const", bufs=1))
        x_pool = stack.enter_context(tc.tile_pool(name="x", bufs=N_PAIRS))
        work = stack.enter_context(tc.tile_pool(name="work", bufs=3))

        wd_sb = const.tile([P, PACK, C], BF16)
        wu_sb = const.tile([P, 2 * HEADS, R], BF16)
        for i in range(WEIGHT_UNITS):
            rows = slice(PAIR * i, PAIR * (i + 1))
            nc.sync.dma_start(out=wd_sb[:, rows, :], in_=w_kv_down.rearrange("(p t) c -> p t c", t=PACK)[:, rows, :])
        x_sb = []
        for s in range(N_PAIRS):
            x_pair = x_pool.tile([P, PAIR, C], BF16)
            nc.sync.dma_start(out=x_pair[:], in_=x_rows[s])
            x_sb.append(x_pair)
        nc.sync.dma_start(out=wu_sb[:], in_=w_kv_up.rearrange("(b p) r -> p b r", p=P))

        cos_sb = const.tile([P, SEQ_TILES, HALF_D], BF16)
        sin_sb = const.tile([P, SEQ_TILES, HALF_D], BF16)
        gain_sb = const.tile([P, HALF_D, 2], BF16)
        nc.scalar.dma_start(
            out=cos_sb[:].rearrange("p (s n) j -> p s n j", n=PAIR),
            in_=freqs_cos.rearrange("(s p n) j -> p s n j", p=P, n=PAIR),
        )
        nc.scalar.dma_start(
            out=sin_sb[:].rearrange("p (s n) j -> p s n j", n=PAIR),
            in_=freqs_sin.rearrange("(s p n) j -> p s n j", p=P, n=PAIR),
        )
        nc.scalar.dma_start(out=gain_sb[:].rearrange("p j e -> p (j e)"), in_=k_norm_w.partition_broadcast(P))

        identity = const.tile([P, P], F32)
        make_identity(nc, identity[:])
        eps = const.tile([P, 1], F32)
        nc.vector.memset(eps[:], EPS)
        table_warmer = const.tile([P, 1], F32)
        nc.scalar.activation(out=table_warmer[:], in_=eps[:], func=ACT.Abs_reciprocal_sqrt)

        signed_gain = const.tile([P, HALF_D, 2], F32)
        nc.vector.tensor_copy(out=signed_gain[:, :, 0], in_=gain_sb[:, :, 0])
        nc.vector.tensor_scalar_mul(out=signed_gain[:, :, 1], in0=gain_sb[:, :, 1], scalar1=-1.0)
        rope_table = const.tile([P, SEQ_TILES, 2, HALF_D, 2], F32)
        table_shape = [P, SEQ_TILES, HALF_D, 2]
        nc.vector.tensor_tensor(
            out=rope_table[:, :, 0],
            in0=cos_sb[:].unsqueeze(3).to_broadcast(table_shape),
            in1=gain_sb[:].unsqueeze(1).to_broadcast(table_shape),
            op=ALU.mult,
        )
        nc.vector.tensor_tensor(
            out=rope_table[:, :, 1],
            in0=sin_sb[:].unsqueeze(3).to_broadcast(table_shape),
            in1=signed_gain[:].unsqueeze(1).to_broadcast(table_shape),
            op=ALU.mult,
        )

        wd_codes = const.tile([P, WEIGHT_UNITS * UNIT_COLS], U32, align_bytes=64)
        wd_scales = const.tile([P, WEIGHT_UNITS * UNIT_COLS], U8, align_bytes=64)
        wu_codes = const.tile([P, WEIGHT_UNITS * UNIT_COLS], U32, align_bytes=64)
        wu_scales = const.tile([P, WEIGHT_UNITS * UNIT_COLS], U8, align_bytes=64)
        x_codes = const.tile([P, N_PAIRS * UNIT_COLS], U32, align_bytes=64)
        x_scales = const.tile([P, N_PAIRS * UNIT_COLS], U8, align_bytes=64)

        unit_blocks = []
        unit_codes = []
        for i in range(WEIGHT_UNITS):
            columns = slice(i * UNIT_COLS, (i + 1) * UNIT_COLS)
            unit_blocks.append([channel_blocks(wd_sb[:, PAIR * i + n, :]) for n in range(PAIR)])
            unit_codes.append((wd_codes[:, columns], wd_scales[:, columns]))
        for s in range(N_PAIRS):
            columns = slice(s * UNIT_COLS, (s + 1) * UNIT_COLS)
            unit_blocks.append([channel_blocks(x_sb[s][:, n, :]) for n in range(PAIR)])
            unit_codes.append((x_codes[:, columns], x_scales[:, columns]))
        for i in range(WEIGHT_UNITS):
            columns = slice(i * UNIT_COLS, (i + 1) * UNIT_COLS)
            unit_blocks.append(
                [feature_blocks(wu_sb[:, 4 * i + 2 * n, :], wu_sb[:, 4 * i + 2 * n + 1, :]) for n in range(PAIR)]
            )
            unit_codes.append((wu_codes[:, columns], wu_scales[:, columns]))
        n_units = len(unit_blocks)

        twin_banks, grouped = {}, {}

        with tc.psum_pool(name="phase1", bufs=4, reuse_waits="tile") as psum:

            def transpose_unit(u):
                twin_banks[u] = []
                for n in range(PAIR):
                    bank = psum.tile([P, 2, 2, P], F32, tag="twins")
                    for a in range(2):
                        for half in range(2):
                            nc.tensor.transpose(bank[:, a, half, :], unit_blocks[u][n][a][half], identity[:])
                    twin_banks[u].append(bank)

            def group_unit(u):
                grouped[u] = work.tile([P, UNIT_COLS * PACK], BF16, align_bytes=64, name="grouped")
                words = grouped[u][:].bitcast(F32).rearrange("q (n a r u) -> q n a r u", n=PAIR, a=2, u=2)
                nc.scalar.copy(out=words[:, 0], in_=twin_banks[u][0][:].rearrange("q a u r -> q a r u"))
                nc.vector.tensor_copy(out=words[:, 1], in_=twin_banks[u][1][:].rearrange("q a u r -> q a r u"))

            def quantise_unit(u):
                codes, scales = unit_codes[u]
                nc.vector.quantize_mx(out=codes.bitcast(FP8X4), scales=scales, in_=grouped[u][:])

            for j in range(n_units + 2):
                if j < n_units:
                    transpose_unit(j)
                if 0 <= j - 1 < n_units:
                    group_unit(j - 1)
                if 0 <= j - 2:
                    quantise_unit(j - 2)

        latent_banks, latent_grouped, latent_codes = {}, {}, {}
        k_banks, v_banks, sum_squares, rstd, products, k_out, v_out = {}, {}, {}, {}, {}, {}, {}

        with tc.psum_pool(name="phase2", bufs=2, reuse_waits="tile") as psum:

            def latent_passes(k):
                latent_banks[k] = psum.tile([P, PACK, P], F32, tag="latent", name="latent_bank")
                for t in range(PACK):
                    for g in range(C_PASSES):
                        nc.tensor.matmul_mx(
                            out=latent_banks[k][:, t, :],
                            lhsT=wd_codes[:, block(t * C_PASSES + g)].bitcast(FP8X4),
                            lhsT_scale=wd_scales[:, block(t * C_PASSES + g)],
                            rhs=x_codes[:, block(k * C_PASSES + g)].bitcast(FP8X4),
                            rhs_scale=x_scales[:, block(k * C_PASSES + g)],
                            start=(g == 0),
                            stop=(g == C_PASSES - 1),
                        )

            def group_latent(k, copy_out):
                if k % PAIR == 0:
                    latent_grouped[k // PAIR] = work.tile([P, PAIR, P, PACK], BF16, align_bytes=64, name="latent_grouped")
                copy_out(out=latent_grouped[k // PAIR][:, k % PAIR], in_=latent_banks[k][:].rearrange("p t r -> p r t"))

            def quantise_latent(s):
                codes = work.tile([P, PAIR * P], U32, align_bytes=64, name="latent_codes")
                scales = work.tile([P, PAIR * P], U8, align_bytes=64, name="latent_scales")
                nc.vector.quantize_mx(
                    out=codes[:].bitcast(FP8X4), scales=scales[:], in_=latent_grouped[s][:].rearrange("p n r t -> p (n r t)")
                )
                latent_codes[s] = (codes, scales)

            def kv_passes(k):
                codes, scales = latent_codes[k // PAIR]
                k_banks[k] = psum.tile([P, HEADS, D], F32, tag="k", bufs=4, name="k_bank")
                v_banks[k] = psum.tile([P, KEY_COLS], F32, tag="v", name="v_bank")
                for bank, first_col in ((k_banks[k][:].rearrange("p h d -> p (h d)"), 0), (v_banks[k][:], KEY_COLS)):
                    nc.tensor.matmul_mx(
                        out=bank,
                        lhsT=codes[:, block(k % PAIR)].bitcast(FP8X4),
                        lhsT_scale=scales[:, block(k % PAIR)],
                        rhs=wu_codes[:, first_col : first_col + KEY_COLS].bitcast(FP8X4),
                        rhs_scale=wu_scales[:, first_col : first_col + KEY_COLS],
                        start=True,
                        stop=True,
                    )

            def sum_key_squares(k):
                squares = work.tile([P, HEADS, D], F32)
                sum_squares[k] = work.tile([P, HEADS], F32, name="sum_squares")
                for h in range(HEADS):
                    nc.scalar.activation(
                        out=squares[:, h], in_=k_banks[k][:, h], func=ACT.Square, accum_out=sum_squares[k][:, h : h + 1]
                    )

            def copy_values(k):
                if k % PAIR == 0:
                    v_out[k // PAIR] = work.tile([P, PAIR, KEY_COLS], F32, name="v_out")
                nc.scalar.copy(out=v_out[k // PAIR][:, k % PAIR, :], in_=v_banks[k][:])
                if k % PAIR == PAIR - 1:
                    nc.sync.dma_start(out=v_rows[k // PAIR], in_=v_out[k // PAIR][:])

            def reciprocal_rms(k):
                rstd[k] = work.tile([P, HEADS], F32, name="rstd")
                nc.scalar.activation(
                    out=rstd[k][:], in_=sum_squares[k][:], func=ACT.Abs_reciprocal_sqrt, scale=1.0 / D, bias=eps[:]
                )

            def multiply_keys(k, heads):
                if k not in products:
                    products[k] = work.tile([P, HEADS, 2, HALF_D, 2], F32, name="products", bufs=4)
                for h in heads:
                    nc.vector.scalar_tensor_tensor(
                        out=products[k][:, h].rearrange("p w j e -> p w (j e)"),
                        in0=k_banks[k][:, h].unsqueeze(1).to_broadcast([P, 2, D]),
                        scalar=rstd[k][:, h : h + 1],
                        in1=rope_table[:, k % SEQ_TILES].rearrange("p w j e -> p w (j e)"),
                        op0=ALU.mult,
                        op1=ALU.mult,
                    )

            def sum_products(k):
                if k % PAIR == 0:
                    k_out[k // PAIR] = work.tile([P, PAIR, KEY_COLS], F32, name="k_out")
                nc.gpsimd.tensor_tensor(
                    out=k_out[k // PAIR][:, k % PAIR, :].rearrange("p (h j e) -> p h j e", h=HEADS, e=2),
                    in0=products[k][:, :, 0],
                    in1=products[k][:, :, 1, :, ::-1],
                    op=ALU.add,
                )
                if k % PAIR == PAIR - 1:
                    nc.sync.dma_start(out=k_rows[k // PAIR], in_=k_out[k // PAIR][:])

            for j in range(N_TILES + 5):
                grouping = j - 1
                finishing = j - 4
                multiplying = j - 5
                vector_groups = 0 <= grouping < N_TILES and grouping % PAIR == PAIR - 1

                if j < N_TILES:
                    latent_passes(j)
                if 0 <= j - 3 < N_TILES:
                    kv_passes(j - 3)
                if 0 <= grouping < N_TILES and not vector_groups:
                    group_latent(grouping, nc.scalar.copy)
                if 0 <= finishing < N_TILES:
                    sum_key_squares(finishing)
                    copy_values(finishing)
                    reciprocal_rms(finishing)
                if vector_groups:
                    group_latent(grouping, nc.vector.tensor_copy)
                if 0 <= multiplying:
                    multiply_keys(multiplying, range(HEADS - 1))
                if vector_groups:
                    quantise_latent(grouping // PAIR)
                if 0 <= multiplying:
                    multiply_keys(multiplying, range(HEADS - 1, HEADS))
                    sum_products(multiplying)
